import numpy as np
import ml_dtypes


def mxq(x, axis, fmt="e4m3"):
    dtype, down = {"e4m3": (ml_dtypes.float8_e4m3fn, 7), "e5m2": (ml_dtypes.float8_e5m2, 14)}[fmt]
    v = np.moveaxis(np.asarray(x, np.float32).astype(ml_dtypes.bfloat16).astype(np.float64), axis, -1)
    blocks = v.reshape(v.shape[:-1] + (-1, 32))
    amax = np.abs(blocks).max(-1, keepdims=True)
    byte = np.maximum(np.where(amax > 0, np.frexp(amax)[1] - 1 + 127, 0) - down, 1)
    scale = np.exp2(byte - 127.0)
    codes = (blocks / scale).astype(np.float32).astype(dtype).astype(np.float64)
    return np.moveaxis((codes * scale).reshape(v.shape), -1, axis)


WIDE = False


def mx_kscale(k):
    if not WIDE:
        return np.ones(k)
    levels = np.array([10, -10, 5, -5, 0])
    a = np.random.permutation(np.resize(levels, k // 512 * 4)).reshape(k // 512, 4)
    idx = np.arange(k)
    return np.exp2(a[idx // 512, idx % 128 // 32])


BF16 = ml_dtypes.bfloat16


def bf(x):
    return np.asarray(x, np.float32).astype(BF16)


def f64(x):
    return np.asarray(x).astype(np.float64)


N, E, G, M, H = 512, 1024, 512, 512, 4
HG = H * G


def setup_inputs():
    r = np.random.standard_normal
    s = mx_kscale(M)
    t = mx_kscale(HG)
    return {"h1": bf(np.maximum(r((N, H, M)), 0.0) * s),
            "W2": bf(r((H, M, G)) * 1.5 / np.sqrt(M) / s[None, :, None] * t.reshape(H, 1, G)),
            "b2": bf(r((H, G)) * 0.2 * t.reshape(H, G)),
            "Ws": bf(r((HG, E)) / np.sqrt(HG) / t[:, None]),
            "q": bf(r((N, E))),
            "rep": bf(r((N, E)))}


def reference(h1, W2, b2, Ws, q, rep):
    ht = f64(h1).transpose(1, 0, 2)
    z2 = (mxq(ht, 2, "e4m3") @ mxq(f64(W2), 1, "e4m3")).transpose(1, 0, 2) + f64(b2)
    update_gate = z2.reshape(N, HG)
    return f64(q) - f64(rep) + (mxq(update_gate, 1, "e4m3") @ mxq(f64(Ws), 0, "e4m3"))

@@ -1,0 +1,155 @@
+from contextlib import ExitStack
+
+import concourse.mybir as mybir
+from concourse.masks import make_identity
+
+FP8X4 = mybir.dt.float8_e4m3fn_x4
+BF16 = mybir.dt.bfloat16
+F32 = mybir.dt.float32
+U32 = mybir.dt.uint32
+U8 = mybir.dt.uint8
+ADD = mybir.AluOpType.add
+SUB = mybir.AluOpType.subtract
+
+P = 128
+N, E, G, M, H = 512, 1024, 512, 512, 4
+A = N // P
+EH = 2
+FLOPS = 2 * N * H * M * G + 2 * N * H * G * E
+
+W2_ON_SCALAR = (1, 3)
+WS_ON_VECTOR = ()
+
+
+def tile_treehopnode_pb_kernel(tc, h1, W2, b2, Ws, q, rep, out):
+    nc = tc.nc
+    with ExitStack() as ctx:
+        keep = ctx.enter_context(tc.tile_pool(name="keep", bufs=1))
+        stage = ctx.enter_context(tc.tile_pool(name="stage", bufs=4))
+        psum = ctx.enter_context(tc.psum_pool(name="psum", bufs=8))
+
+        ident = keep.tile([P, P], F32, name="ident")
+        make_identity(nc, ident[:])
+        bias = keep.tile([P, H, 4], BF16, name="bias")
+        nc.scalar.dma_start(out=bias[:], in_=b2.rearrange("h (p t) -> p h t", t=4))
+
+        h1_raw = [keep.tile([P, H * M], BF16, name="h1_raw%d" % a) for a in range(A)]
+        w2_raw = [keep.tile([P, 4, G], BF16, name="w2_raw%d" % h) for h in range(H)]
+        ws_raw = [keep.tile([P, 4, E], BF16, name="ws_raw%d" % h) for h in range(H)]
+        q_sb = keep.tile([P, A, E], BF16, name="q_sb")
+        rep_sb = keep.tile([P, A, E], BF16, name="rep_sb")
+        h1_view = h1.rearrange("(p a) h m -> p a (h m)", a=A)
+        for i in range(4):
+            nc.sync.dma_start(out=h1_raw[i][:], in_=h1_view[:, i, :])
+            nc.sync.dma_start(
+                out=w2_raw[i][:].rearrange("p (u e) g -> p u (e g)", u=2),
+                in_=W2[i].rearrange("(u p e) g -> p u (e g)", u=2, e=2),
+            )
+        for h in range(H):
+            nc.sync.dma_start(
+                out=ws_raw[h][:].rearrange("p t e -> p (t e)"),
+                in_=Ws[h * G : (h + 1) * G, :].rearrange("(p t) e -> p (t e)", t=4),
+            )
+        nc.sync.dma_start(out=q_sb[:].rearrange("p a e -> p (a e)"), in_=q.rearrange("(p a) e -> p (a e)", a=A))
+        nc.sync.dma_start(out=rep_sb[:].rearrange("p a e -> p (a e)"), in_=rep.rearrange("(p a) e -> p (a e)", a=A))
+
+        h1_codes = [keep.tile([P, H * P], U32, name="h1_codes%d" % a, align_bytes=64) for a in range(A)]
+        h1_scales = [keep.tile([P, H * P], U8, name="h1_scales%d" % a, align_bytes=64) for a in range(A)]
+        w2_codes = [keep.tile([P, G], U32, name="w2_codes%d" % h, align_bytes=64) for h in range(H)]
+        w2_scales = [keep.tile([P, G], U8, name="w2_scales%d" % h, align_bytes=64) for h in range(H)]
+        z_codes = [keep.tile([P, H * P], U32, name="z_codes%d" % a, align_bytes=64) for a in range(A)]
+        z_scales = [keep.tile([P, H * P], U8, name="z_scales%d" % a, align_bytes=64) for a in range(A)]
+        ws_codes = [[keep.tile([P, 512], U32, name="ws_codes%d_%d" % (eh, h), align_bytes=64) for h in range(H)] for eh in range(EH)]
+        ws_scales = [[keep.tile([P, 512], U8, name="ws_scales%d_%d" % (eh, h), align_bytes=64) for h in range(H)] for eh in range(EH)]
+        resid = [keep.tile([P, E], F32, name="resid%d" % a) for a in range(A)]
+
+        def prepare_h1(a):
+            words = h1_raw[a][:].bitcast(F32)
+            grouped = stage.tile([P, 2048], BF16, name="h1_grouped", tag="grouped", align_bytes=64)
+            grouped_words = grouped[:].bitcast(F32).rearrange("p (h r u) -> p h r u", h=H, u=2)
+            for hp in range(2):
+                bank = psum.tile([P, 2, 2, P], F32, name="tp_bank", tag="bank")
+                for hh in range(2):
+                    for u in range(2):
+                        c0 = 256 * (2 * hp + hh) + 128 * u
+                        nc.tensor.transpose(bank[:, hh, u, :], words[:, c0 : c0 + P], ident[:])
+                nc.scalar.copy(
+                    out=grouped_words[:, 2 * hp : 2 * hp + 2, :, :],
+                    in_=bank[:].rearrange("p hh u r -> p hh r u"),
+                )
+            nc.vector.quantize_mx(out=h1_codes[a][:].bitcast(FP8X4), scales=h1_scales[a][:], in_=grouped[:])
+
+        def prepare_w2(h):
+            grouped = stage.tile([P, 2048], BF16, name="w2_grouped", tag="grouped", align_bytes=64)
+            dst = grouped[:].rearrange("p (t c j) -> p c j t", t=4, j=4)
+            src = w2_raw[h][:].rearrange("p j (c t) -> p c j t", t=4)
+            if h in W2_ON_SCALAR:
+                nc.scalar.copy(out=dst, in_=src)
+            else:
+                nc.vector.tensor_copy(out=dst, in_=src)
+            nc.vector.quantize_mx(out=w2_codes[h][:].bitcast(FP8X4), scales=w2_scales[h][:], in_=grouped[:])
+
+        def stage1(h, a):
+            bank = psum.tile([P, 4, P], F32, name="s1_bank", tag="bank")
+            cols = slice(h * P, (h + 1) * P)
+            for t in range(4):
+                g_cols = slice(t * P, (t + 1) * P)
+                nc.tensor.matmul_mx(
+                    out=bank[:, t, :],
+                    lhsT=w2_codes[h][:, g_cols].bitcast(FP8X4),
+                    lhsT_scale=w2_scales[h][:, g_cols],
+                    rhs=h1_codes[a][:, cols].bitcast(FP8X4),
+                    rhs_scale=h1_scales[a][:, cols],
+                    start=True,
+                    stop=True,
+                )
+            z_grouped = stage.tile([P, P, 4], BF16, name="z_grouped", tag="z_grouped", align_bytes=64)
+            nc.vector.tensor_tensor(
+                out=z_grouped[:],
+                in0=bank[:].rearrange("p t r -> p r t"),
+                in1=bias[:, h, :].unsqueeze(1).to_broadcast([P, P, 4]),
+                op=ADD,
+            )
+            nc.vector.quantize_mx(
+                out=z_codes[a][:, cols].bitcast(FP8X4),
+                scales=z_scales[a][:, cols],
+                in_=z_grouped[:].rearrange("p r t -> p (r t)"),
+            )
+
+        for i in range(4):
+            prepare_h1(i)
+            prepare_w2(i)
+            for h in range(i):
+                stage1(h, i)
+            for a in range(i + 1):
+                stage1(i, a)
+
+        out_view = out.rearrange("(p a) e -> p a e", a=A)
+        for eh in range(EH):
+            e_cols = slice(eh * 512, (eh + 1) * 512)
+            banks = [psum.tile([P, 512], F32, name="out_bank%d" % a, tag="bank") for a in range(A)]
+            for h in range(H):
+                grouped = stage.tile([P, 2048], BF16, name="ws_grouped", tag="grouped", align_bytes=64)
+                dst = grouped[:].rearrange("p (c i t) -> p c t i", i=4, t=4)
+                src = ws_raw[h][:, :, e_cols].rearrange("p t (c i) -> p c t i", i=4)
+                if (eh, h) in WS_ON_VECTOR:
+                    nc.vector.tensor_copy(out=dst, in_=src)
+                else:
+                    nc.scalar.copy(out=dst, in_=src)
+                nc.vector.quantize_mx(out=ws_codes[eh][h][:].bitcast(FP8X4), scales=ws_scales[eh][h][:], in_=grouped[:])
+                for a in range(A):
+                    cols = slice(h * P, (h + 1) * P)
+                    nc.tensor.matmul_mx(
+                        out=banks[a][:],
+                        lhsT=z_codes[a][:, cols].bitcast(FP8X4),
+                        lhsT_scale=z_scales[a][:, cols],
+                        rhs=ws_codes[eh][h][:].bitcast(FP8X4),
+                        rhs_scale=ws_scales[eh][h][:],
+                        start=(h == 0),
+                        stop=(h == H - 1),
+                    )
+            for a in range(A):
+                if eh == 0:
+                    nc.vector.tensor_tensor(out=resid[a][:], in0=q_sb[:, a, :], in1=rep_sb[:, a, :], op=SUB)
+                nc.vector.tensor_tensor(out=resid[a][:, e_cols], in0=banks[a][:], in1=resid[a][:, e_cols], op=ADD)
+                nc.sync.dma_start(out=out_view[:, a, e_cols], in_=resid[a][:, e_cols])

@@ -17,34 +17,31 @@ A = N // P
 EH = 2
 FLOPS = 2 * N * H * M * G + 2 * N * H * G * E
 
-W2_ON_SCALAR = (1, 3)
-WS_ON_VECTOR = ()
-
 
 def tile_treehopnode_pb_kernel(tc, h1, W2, b2, Ws, q, rep, out):
     nc = tc.nc
     with ExitStack() as ctx:
         keep = ctx.enter_context(tc.tile_pool(name="keep", bufs=1))
-        stage = ctx.enter_context(tc.tile_pool(name="stage", bufs=4))
-        psum = ctx.enter_context(tc.psum_pool(name="psum", bufs=8))
+        psum = ctx.enter_context(tc.psum_pool(name="psum", bufs=1))
+        ctx.enter_context(tc.manual_schedule())
 
         ident = keep.tile([P, P], F32, name="ident")
         make_identity(nc, ident[:])
         bias = keep.tile([P, H, 4], BF16, name="bias")
         nc.scalar.dma_start(out=bias[:], in_=b2.rearrange("h (p t) -> p h t", t=4))
 
-        h1_raw = [keep.tile([P, H * M], BF16, name="h1_raw%d" % a) for a in range(A)]
+        h1_raw = [keep.tile([P, A, M], BF16, name="h1_raw%d" % h) for h in range(H)]
         w2_raw = [keep.tile([P, 4, G], BF16, name="w2_raw%d" % h) for h in range(H)]
         ws_raw = [keep.tile([P, 4, E], BF16, name="ws_raw%d" % h) for h in range(H)]
         q_sb = keep.tile([P, A, E], BF16, name="q_sb")
         rep_sb = keep.tile([P, A, E], BF16, name="rep_sb")
-        h1_view = h1.rearrange("(p a) h m -> p a (h m)", a=A)
-        for i in range(4):
-            nc.sync.dma_start(out=h1_raw[i][:], in_=h1_view[:, i, :])
+        h1_view = h1.rearrange("(p a) h m -> p a h m", a=A)
+        for h in range(H):
             nc.sync.dma_start(
-                out=w2_raw[i][:].rearrange("p (u e) g -> p u (e g)", u=2),
-                in_=W2[i].rearrange("(u p e) g -> p u (e g)", u=2, e=2),
+                out=w2_raw[h][:].rearrange("p (u e) g -> p u (e g)", u=2),
+                in_=W2[h].rearrange("(u p e) g -> p u (e g)", u=2, e=2),
             )
+            nc.sync.dma_start(out=h1_raw[h][:], in_=h1_view[:, :, h, :])
         for h in range(H):
             nc.sync.dma_start(
                 out=ws_raw[h][:].rearrange("p t e -> p (t e)"),
@@ -53,103 +50,139 @@ def tile_treehopnode_pb_kernel(tc, h1, W2, b2, Ws, q, rep, out):
         nc.sync.dma_start(out=q_sb[:].rearrange("p a e -> p (a e)"), in_=q.rearrange("(p a) e -> p (a e)", a=A))
         nc.sync.dma_start(out=rep_sb[:].rearrange("p a e -> p (a e)"), in_=rep.rearrange("(p a) e -> p (a e)", a=A))
 
-        h1_codes = [keep.tile([P, H * P], U32, name="h1_codes%d" % a, align_bytes=64) for a in range(A)]
-        h1_scales = [keep.tile([P, H * P], U8, name="h1_scales%d" % a, align_bytes=64) for a in range(A)]
-        w2_codes = [keep.tile([P, G], U32, name="w2_codes%d" % h, align_bytes=64) for h in range(H)]
-        w2_scales = [keep.tile([P, G], U8, name="w2_scales%d" % h, align_bytes=64) for h in range(H)]
-        z_codes = [keep.tile([P, H * P], U32, name="z_codes%d" % a, align_bytes=64) for a in range(A)]
-        z_scales = [keep.tile([P, H * P], U8, name="z_scales%d" % a, align_bytes=64) for a in range(A)]
-        ws_codes = [[keep.tile([P, 512], U32, name="ws_codes%d_%d" % (eh, h), align_bytes=64) for h in range(H)] for eh in range(EH)]
-        ws_scales = [[keep.tile([P, 512], U8, name="ws_scales%d_%d" % (eh, h), align_bytes=64) for h in range(H)] for eh in range(EH)]
+        def words_and_plane(name):
+            return (
+                keep.tile([P, 512], U32, name=name + "_codes", align_bytes=64),
+                keep.tile([P, 512], U8, name=name + "_scales", align_bytes=64),
+            )
+
+        h1_mx = [words_and_plane("h1_%d" % h) for h in range(H)]
+        w2_mx = [words_and_plane("w2_%d" % h) for h in range(H)]
+        z_mx = [words_and_plane("z_%d" % h) for h in range(H)]
+        ws_mx = [[words_and_plane("ws_%d_%d" % (e, h)) for h in range(H)] for e in range(EH)]
         resid = [keep.tile([P, E], F32, name="resid%d" % a) for a in range(A)]
 
-        def prepare_h1(a):
-            words = h1_raw[a][:].bitcast(F32)
-            grouped = stage.tile([P, 2048], BF16, name="h1_grouped", tag="grouped", align_bytes=64)
-            grouped_words = grouped[:].bitcast(F32).rearrange("p (h r u) -> p h r u", h=H, u=2)
-            for hp in range(2):
-                bank = psum.tile([P, 2, 2, P], F32, name="tp_bank", tag="bank")
-                for hh in range(2):
+        def grouped_tile(slot):
+            return keep.tile([P, 2048], BF16, name="grouped", tag="grouped%d" % slot, align_bytes=64)
+
+        def bank_tile(shape, bank):
+            return psum.tile(shape, F32, name="bank", tag="bank%d" % bank)
+
+        def quantise(mx, grouped):
+            nc.vector.quantize_mx(out=mx[0][:].bitcast(FP8X4), scales=mx[1][:], in_=grouped[:])
+
+        h1_grouped = {}
+        w2_grouped = {}
+        z_grouped = {}
+        ws_grouped = {}
+        out_banks = {}
+
+        def transpose_h1(h):
+            words = h1_raw[h][:].rearrange("p a m -> p (a m)").bitcast(F32)
+            h1_grouped[h] = grouped_tile(h)
+            grouped_words = h1_grouped[h][:].bitcast(F32).rearrange("p (a r u) -> p a r u", a=A, u=2)
+            for b in range(2):
+                bank = bank_tile([P, 2, 2, P], (2 * h + b) % 4)
+                for aa in range(2):
                     for u in range(2):
-                        c0 = 256 * (2 * hp + hh) + 128 * u
-                        nc.tensor.transpose(bank[:, hh, u, :], words[:, c0 : c0 + P], ident[:])
+                        c0 = 256 * (2 * b + aa) + 128 * u
+                        nc.tensor.transpose(bank[:, aa, u, :], words[:, c0 : c0 + P], ident[:])
                 nc.scalar.copy(
-                    out=grouped_words[:, 2 * hp : 2 * hp + 2, :, :],
-                    in_=bank[:].rearrange("p hh u r -> p hh r u"),
+                    out=grouped_words[:, 2 * b : 2 * b + 2, :, :],
+                    in_=bank[:].rearrange("p aa u r -> p aa r u"),
                 )
-            nc.vector.quantize_mx(out=h1_codes[a][:].bitcast(FP8X4), scales=h1_scales[a][:], in_=grouped[:])
 
-        def prepare_w2(h):
-            grouped = stage.tile([P, 2048], BF16, name="w2_grouped", tag="grouped", align_bytes=64)
-            dst = grouped[:].rearrange("p (t c j) -> p c j t", t=4, j=4)
+        def regroup_w2(h, engine):
+            w2_grouped[h] = grouped_tile(4 + h)
+            dst = w2_grouped[h][:].rearrange("p (t c j) -> p c j t", t=4, j=4)
             src = w2_raw[h][:].rearrange("p j (c t) -> p c j t", t=4)
-            if h in W2_ON_SCALAR:
-                nc.scalar.copy(out=dst, in_=src)
-            else:
+            if engine == "vector":
                 nc.vector.tensor_copy(out=dst, in_=src)
-            nc.vector.quantize_mx(out=w2_codes[h][:].bitcast(FP8X4), scales=w2_scales[h][:], in_=grouped[:])
+            else:
+                nc.scalar.copy(out=dst, in_=src)
 
-        def stage1(h, a):
-            bank = psum.tile([P, 4, P], F32, name="s1_bank", tag="bank")
-            cols = slice(h * P, (h + 1) * P)
-            for t in range(4):
-                g_cols = slice(t * P, (t + 1) * P)
-                nc.tensor.matmul_mx(
-                    out=bank[:, t, :],
-                    lhsT=w2_codes[h][:, g_cols].bitcast(FP8X4),
-                    lhsT_scale=w2_scales[h][:, g_cols],
-                    rhs=h1_codes[a][:, cols].bitcast(FP8X4),
-                    rhs_scale=h1_scales[a][:, cols],
-                    start=True,
-                    stop=True,
+        def stage1(h):
+            z_grouped[h] = grouped_tile(8 + h)
+            z_view = z_grouped[h][:].rearrange("p (a r t) -> p a r t", a=A, t=4)
+            for a in range(A):
+                bank = bank_tile([P, 4, P], 4 + a)
+                cols = slice(a * P, (a + 1) * P)
+                for t in range(4):
+                    g_cols = slice(t * P, (t + 1) * P)
+                    nc.tensor.matmul_mx(
+                        out=bank[:, t, :],
+                        lhsT=w2_mx[h][0][:, g_cols].bitcast(FP8X4),
+                        lhsT_scale=w2_mx[h][1][:, g_cols],
+                        rhs=h1_mx[h][0][:, cols].bitcast(FP8X4),
+                        rhs_scale=h1_mx[h][1][:, cols],
+                        start=True,
+                        stop=True,
+                    )
+                nc.vector.tensor_tensor(
+                    out=z_view[:, a, :, :],
+                    in0=bank[:].rearrange("p t r -> p r t"),
+                    in1=bias[:, h, :].unsqueeze(1).to_broadcast([P, P, 4]),
+                    op=ADD,
                 )
-            z_grouped = stage.tile([P, P, 4], BF16, name="z_grouped", tag="z_grouped", align_bytes=64)
-            nc.vector.tensor_tensor(
-                out=z_grouped[:],
-                in0=bank[:].rearrange("p t r -> p r t"),
-                in1=bias[:, h, :].unsqueeze(1).to_broadcast([P, P, 4]),
-                op=ADD,
-            )
-            nc.vector.quantize_mx(
-                out=z_codes[a][:, cols].bitcast(FP8X4),
-                scales=z_scales[a][:, cols],
-                in_=z_grouped[:].rearrange("p r t -> p (r t)"),
-            )
+            quantise(z_mx[h], z_grouped[h])
 
-        for i in range(4):
-            prepare_h1(i)
-            prepare_w2(i)
-            for h in range(i):
-                stage1(h, i)
-            for a in range(i + 1):
-                stage1(i, a)
+        def regroup_ws(e, h):
+            ws_grouped[(e, h)] = grouped_tile(12 + h if e == 0 else h)
+            dst = ws_grouped[(e, h)][:].rearrange("p (c i t) -> p c t i", i=4, t=4)
+            src = ws_raw[h][:, :, e * 512 : (e + 1) * 512].rearrange("p t (c i) -> p c t i", i=4)
+            nc.scalar.copy(out=dst, in_=src)
+
+        def stage2(e, h):
+            for a in range(A):
+                if h == 0:
+                    out_banks[(e, a)] = bank_tile([P, 512], 4 * e + a)
+                cols = slice(a * P, (a + 1) * P)
+                nc.tensor.matmul_mx(
+                    out=out_banks[(e, a)][:],
+                    lhsT=z_mx[h][0][:, cols].bitcast(FP8X4),
+                    lhsT_scale=z_mx[h][1][:, cols],
+                    rhs=ws_mx[e][h][0][:].bitcast(FP8X4),
+                    rhs_scale=ws_mx[e][h][1][:],
+                    start=(h == 0),
+                    stop=(h == H - 1),
+                )
 
         out_view = out.rearrange("(p a) e -> p a e", a=A)
-        for eh in range(EH):
-            e_cols = slice(eh * 512, (eh + 1) * 512)
-            banks = [psum.tile([P, 512], F32, name="out_bank%d" % a, tag="bank") for a in range(A)]
-            for h in range(H):
-                grouped = stage.tile([P, 2048], BF16, name="ws_grouped", tag="grouped", align_bytes=64)
-                dst = grouped[:].rearrange("p (c i t) -> p c t i", i=4, t=4)
-                src = ws_raw[h][:, :, e_cols].rearrange("p t (c i) -> p c t i", i=4)
-                if (eh, h) in WS_ON_VECTOR:
-                    nc.vector.tensor_copy(out=dst, in_=src)
-                else:
-                    nc.scalar.copy(out=dst, in_=src)
-                nc.vector.quantize_mx(out=ws_codes[eh][h][:].bitcast(FP8X4), scales=ws_scales[eh][h][:], in_=grouped[:])
-                for a in range(A):
-                    cols = slice(h * P, (h + 1) * P)
-                    nc.tensor.matmul_mx(
-                        out=banks[a][:],
-                        lhsT=z_codes[a][:, cols].bitcast(FP8X4),
-                        lhsT_scale=z_scales[a][:, cols],
-                        rhs=ws_codes[eh][h][:].bitcast(FP8X4),
-                        rhs_scale=ws_scales[eh][h][:],
-                        start=(h == 0),
-                        stop=(h == H - 1),
-                    )
+
+        def finish(e):
+            e_cols = slice(e * 512, (e + 1) * 512)
             for a in range(A):
-                if eh == 0:
-                    nc.vector.tensor_tensor(out=resid[a][:], in0=q_sb[:, a, :], in1=rep_sb[:, a, :], op=SUB)
-                nc.vector.tensor_tensor(out=resid[a][:, e_cols], in0=banks[a][:], in1=resid[a][:, e_cols], op=ADD)
+                nc.vector.tensor_tensor(out=resid[a][:, e_cols], in0=out_banks[(e, a)][:], in1=resid[a][:, e_cols], op=ADD)
                 nc.sync.dma_start(out=out_view[:, a, e_cols], in_=resid[a][:, e_cols])
+
+        transpose_h1(0)
+        regroup_w2(0, "vector")
+        quantise(w2_mx[0], w2_grouped[0])
+        regroup_w2(1, "vector")
+        quantise(h1_mx[0], h1_grouped[0])
+        quantise(w2_mx[1], w2_grouped[1])
+        transpose_h1(1)
+        stage1(0)
+        regroup_w2(2, "scalar")
+        transpose_h1(2)
+        regroup_w2(3, "scalar")
+        transpose_h1(3)
+        quantise(h1_mx[1], h1_grouped[1])
+        quantise(w2_mx[2], w2_grouped[2])
+        quantise(h1_mx[2], h1_grouped[2])
+        stage1(1)
+        quantise(w2_mx[3], w2_grouped[3])
+        quantise(h1_mx[3], h1_grouped[3])
+        stage1(2)
+        stage1(3)
+        for h in range(H):
+            regroup_ws(0, h)
+            quantise(ws_mx[0][h], ws_grouped[(0, h)])
+            stage2(0, h)
+        for h in range(H):
+            nc.vector.tensor_tensor(out=resid[h][:], in0=q_sb[:, h, :], in1=rep_sb[:, h, :], op=SUB)
+            regroup_ws(1, h)
+            quantise(ws_mx[1][h], ws_grouped[(1, h)])
+            stage2(1, h)
+        finish(0)
+        finish(1)

@@ -9,180 +9,167 @@ F32 = mybir.dt.float32
 U32 = mybir.dt.uint32
 U8 = mybir.dt.uint8
 ADD = mybir.AluOpType.add
-SUB = mybir.AluOpType.subtract
+SUBTRACT = mybir.AluOpType.subtract
 
 P = 128
+PACK = 4
 N, E, G, M, H = 512, 1024, 512, 512, 4
 A = N // P
-EH = 2
+N_TILE = 512
+E_HALVES = E // N_TILE
 FLOPS = 2 * N * H * M * G + 2 * N * H * G * E
+
+W2_HEADS_ON_VECTOR = (0, 1)
 
 
 def tile_treehopnode_pb_kernel(tc, h1, W2, b2, Ws, q, rep, out):
     nc = tc.nc
     with ExitStack() as ctx:
-        keep = ctx.enter_context(tc.tile_pool(name="keep", bufs=1))
+        sbuf = ctx.enter_context(tc.tile_pool(name="sbuf", bufs=1))
         psum = ctx.enter_context(tc.psum_pool(name="psum", bufs=1))
         ctx.enter_context(tc.manual_schedule())
 
-        ident = keep.tile([P, P], F32, name="ident")
-        make_identity(nc, ident[:])
-        bias = keep.tile([P, H, 4], BF16, name="bias")
-        nc.scalar.dma_start(out=bias[:], in_=b2.rearrange("h (p t) -> p h t", t=4))
+        identity = sbuf.tile([P, P], F32, name="identity")
+        make_identity(nc, identity[:])
+        bias = sbuf.tile([P, H, PACK], BF16, name="bias")
+        nc.scalar.dma_start(out=bias[:], in_=b2.rearrange("h (c t) -> c h t", t=PACK))
 
-        h1_raw = [keep.tile([P, A, M], BF16, name="h1_raw%d" % h) for h in range(H)]
-        w2_raw = [keep.tile([P, 4, G], BF16, name="w2_raw%d" % h) for h in range(H)]
-        ws_raw = [keep.tile([P, 4, E], BF16, name="ws_raw%d" % h) for h in range(H)]
-        q_sb = keep.tile([P, A, E], BF16, name="q_sb")
-        rep_sb = keep.tile([P, A, E], BF16, name="rep_sb")
-        h1_view = h1.rearrange("(p a) h m -> p a h m", a=A)
+        h1_raw = [sbuf.tile([P, A, M], BF16, name="h1_raw%d" % h) for h in range(H)]
+        w2_raw = [sbuf.tile([P, PACK, G], BF16, name="w2_raw%d" % h) for h in range(H)]
+        ws_raw = [sbuf.tile([P, PACK, E], BF16, name="ws_raw%d" % h) for h in range(H)]
+        q_raw = sbuf.tile([P, A, E], BF16, name="q_raw")
+        rep_raw = sbuf.tile([P, A, E], BF16, name="rep_raw")
+        h1_by_tile = h1.rearrange("(r a) h m -> r a h m", a=A)
         for h in range(H):
+            nc.sync.dma_start(out=h1_raw[h][:], in_=h1_by_tile[:, :, h, :])
             nc.sync.dma_start(
                 out=w2_raw[h][:].rearrange("p (u e) g -> p u (e g)", u=2),
                 in_=W2[h].rearrange("(u p e) g -> p u (e g)", u=2, e=2),
             )
-            nc.sync.dma_start(out=h1_raw[h][:], in_=h1_view[:, :, h, :])
         for h in range(H):
             nc.sync.dma_start(
                 out=ws_raw[h][:].rearrange("p t e -> p (t e)"),
-                in_=Ws[h * G : (h + 1) * G, :].rearrange("(p t) e -> p (t e)", t=4),
+                in_=Ws[h * G : (h + 1) * G, :].rearrange("(p t) e -> p (t e)", t=PACK),
             )
-        nc.sync.dma_start(out=q_sb[:].rearrange("p a e -> p (a e)"), in_=q.rearrange("(p a) e -> p (a e)", a=A))
-        nc.sync.dma_start(out=rep_sb[:].rearrange("p a e -> p (a e)"), in_=rep.rearrange("(p a) e -> p (a e)", a=A))
+        nc.sync.dma_start(out=q_raw[:].rearrange("r a e -> r (a e)"), in_=q.rearrange("(r a) e -> r (a e)", a=A))
+        nc.sync.dma_start(out=rep_raw[:].rearrange("r a e -> r (a e)"), in_=rep.rearrange("(r a) e -> r (a e)", a=A))
 
-        def words_and_plane(name):
-            return (
-                keep.tile([P, 512], U32, name=name + "_codes", align_bytes=64),
-                keep.tile([P, 512], U8, name=name + "_scales", align_bytes=64),
+        def mx_operand(name):
+            return {
+                "grouped": sbuf.tile([P, N_TILE * PACK], BF16, name=name + "_grouped", align_bytes=64),
+                "words": sbuf.tile([P, N_TILE], U32, name=name + "_words", align_bytes=64),
+                "scales": sbuf.tile([P, N_TILE], U8, name=name + "_scales", align_bytes=64),
+            }
+
+        h1_mx = [mx_operand("h1_%d" % h) for h in range(H)]
+        w2_mx = [mx_operand("w2_%d" % h) for h in range(H)]
+        z_mx = [mx_operand("z_%d" % h) for h in range(H)]
+        ws_mx = [[mx_operand("ws_%d_%d" % (half, h)) for h in range(H)] for half in range(E_HALVES)]
+        residual = [sbuf.tile([P, E], F32, name="residual%d" % a) for a in range(A)]
+
+        def quantise(operand):
+            nc.vector.quantize_mx(
+                out=operand["words"][:].bitcast(FP8X4), scales=operand["scales"][:], in_=operand["grouped"][:]
             )
 
-        h1_mx = [words_and_plane("h1_%d" % h) for h in range(H)]
-        w2_mx = [words_and_plane("w2_%d" % h) for h in range(H)]
-        z_mx = [words_and_plane("z_%d" % h) for h in range(H)]
-        ws_mx = [[words_and_plane("ws_%d_%d" % (e, h)) for h in range(H)] for e in range(EH)]
-        resid = [keep.tile([P, E], F32, name="resid%d" % a) for a in range(A)]
+        def matmul_mx(acc, stationary, moving, stationary_cols, moving_cols, start, stop):
+            nc.tensor.matmul_mx(
+                out=acc,
+                lhsT=stationary["words"][:, stationary_cols].bitcast(FP8X4),
+                lhsT_scale=stationary["scales"][:, stationary_cols],
+                rhs=moving["words"][:, moving_cols].bitcast(FP8X4),
+                rhs_scale=moving["scales"][:, moving_cols],
+                start=start,
+                stop=stop,
+            )
 
-        def grouped_tile(slot):
-            return keep.tile([P, 2048], BF16, name="grouped", tag="grouped%d" % slot, align_bytes=64)
-
-        def bank_tile(shape, bank):
+        def psum_bank(shape, bank):
             return psum.tile(shape, F32, name="bank", tag="bank%d" % bank)
 
-        def quantise(mx, grouped):
-            nc.vector.quantize_mx(out=mx[0][:].bitcast(FP8X4), scales=mx[1][:], in_=grouped[:])
+        def prepare_head(h):
+            pairs = h1_raw[h][:].rearrange("r a m -> r (a m)").bitcast(F32)
+            grouped_pairs = h1_mx[h]["grouped"][:].bitcast(F32).rearrange("p (a r u) -> p a r u", a=A, u=2)
+            for b in range(2):
+                bank = psum_bank([P, 2, 2, P], (2 * h + b) % 4)
+                for i in range(2):
+                    for u in range(2):
+                        first = (M // 2) * (2 * b + i) + P * u
+                        nc.tensor.transpose(bank[:, i, u, :], pairs[:, first : first + P], identity[:])
+                nc.scalar.copy(
+                    out=grouped_pairs[:, 2 * b : 2 * b + 2, :, :], in_=bank[:].rearrange("p i u r -> p i r u")
+                )
+            regrouped = w2_mx[h]["grouped"][:].rearrange("p (t c j) -> p c j t", t=PACK, j=PACK)
+            rows = w2_raw[h][:].rearrange("p j (c t) -> p c j t", t=PACK)
+            if h in W2_HEADS_ON_VECTOR:
+                nc.vector.tensor_copy(out=regrouped, in_=rows)
+            else:
+                nc.scalar.copy(out=regrouped, in_=rows)
 
-        h1_grouped = {}
-        w2_grouped = {}
-        z_grouped = {}
-        ws_grouped = {}
+        def quantise_head(h):
+            quantise(h1_mx[h])
+            quantise(w2_mx[h])
+
+        def stage1(h, a):
+            bank = psum_bank([P, PACK, P], 4 + a)
+            for t in range(PACK):
+                matmul_mx(
+                    bank[:, t, :], w2_mx[h], h1_mx[h], slice(t * P, (t + 1) * P), slice(a * P, (a + 1) * P), True, True
+                )
+            nc.vector.tensor_tensor(
+                out=z_mx[h]["grouped"][:].rearrange("c (a r t) -> c a r t", a=A, t=PACK)[:, a, :, :],
+                in0=bank[:].rearrange("c t r -> c r t"),
+                in1=bias[:, h, :].unsqueeze(1).to_broadcast([P, P, PACK]),
+                op=ADD,
+            )
+
+        def regroup_ws(half, h):
+            nc.scalar.copy(
+                out=ws_mx[half][h]["grouped"][:].rearrange("p (c i t) -> p c t i", i=4, t=PACK),
+                in_=ws_raw[h][:, :, half * N_TILE : (half + 1) * N_TILE].rearrange("p t (c i) -> p c t i", i=4),
+            )
+
         out_banks = {}
 
-        def transpose_h1(h):
-            words = h1_raw[h][:].rearrange("p a m -> p (a m)").bitcast(F32)
-            h1_grouped[h] = grouped_tile(h)
-            grouped_words = h1_grouped[h][:].bitcast(F32).rearrange("p (a r u) -> p a r u", a=A, u=2)
-            for b in range(2):
-                bank = bank_tile([P, 2, 2, P], (2 * h + b) % 4)
-                for aa in range(2):
-                    for u in range(2):
-                        c0 = 256 * (2 * b + aa) + 128 * u
-                        nc.tensor.transpose(bank[:, aa, u, :], words[:, c0 : c0 + P], ident[:])
-                nc.scalar.copy(
-                    out=grouped_words[:, 2 * b : 2 * b + 2, :, :],
-                    in_=bank[:].rearrange("p aa u r -> p aa r u"),
-                )
-
-        def regroup_w2(h, engine):
-            w2_grouped[h] = grouped_tile(4 + h)
-            dst = w2_grouped[h][:].rearrange("p (t c j) -> p c j t", t=4, j=4)
-            src = w2_raw[h][:].rearrange("p j (c t) -> p c j t", t=4)
-            if engine == "vector":
-                nc.vector.tensor_copy(out=dst, in_=src)
-            else:
-                nc.scalar.copy(out=dst, in_=src)
-
-        def stage1(h):
-            z_grouped[h] = grouped_tile(8 + h)
-            z_view = z_grouped[h][:].rearrange("p (a r t) -> p a r t", a=A, t=4)
-            for a in range(A):
-                bank = bank_tile([P, 4, P], 4 + a)
-                cols = slice(a * P, (a + 1) * P)
-                for t in range(4):
-                    g_cols = slice(t * P, (t + 1) * P)
-                    nc.tensor.matmul_mx(
-                        out=bank[:, t, :],
-                        lhsT=w2_mx[h][0][:, g_cols].bitcast(FP8X4),
-                        lhsT_scale=w2_mx[h][1][:, g_cols],
-                        rhs=h1_mx[h][0][:, cols].bitcast(FP8X4),
-                        rhs_scale=h1_mx[h][1][:, cols],
-                        start=True,
-                        stop=True,
-                    )
-                nc.vector.tensor_tensor(
-                    out=z_view[:, a, :, :],
-                    in0=bank[:].rearrange("p t r -> p r t"),
-                    in1=bias[:, h, :].unsqueeze(1).to_broadcast([P, P, 4]),
-                    op=ADD,
-                )
-            quantise(z_mx[h], z_grouped[h])
-
-        def regroup_ws(e, h):
-            ws_grouped[(e, h)] = grouped_tile(12 + h if e == 0 else h)
-            dst = ws_grouped[(e, h)][:].rearrange("p (c i t) -> p c t i", i=4, t=4)
-            src = ws_raw[h][:, :, e * 512 : (e + 1) * 512].rearrange("p t (c i) -> p c t i", i=4)
-            nc.scalar.copy(out=dst, in_=src)
-
-        def stage2(e, h):
+        def stage2(half, h):
             for a in range(A):
                 if h == 0:
-                    out_banks[(e, a)] = bank_tile([P, 512], 4 * e + a)
-                cols = slice(a * P, (a + 1) * P)
-                nc.tensor.matmul_mx(
-                    out=out_banks[(e, a)][:],
-                    lhsT=z_mx[h][0][:, cols].bitcast(FP8X4),
-                    lhsT_scale=z_mx[h][1][:, cols],
-                    rhs=ws_mx[e][h][0][:].bitcast(FP8X4),
-                    rhs_scale=ws_mx[e][h][1][:],
-                    start=(h == 0),
-                    stop=(h == H - 1),
+                    out_banks[(half, a)] = psum_bank([P, N_TILE], 4 * half + a)
+                matmul_mx(
+                    out_banks[(half, a)][:], z_mx[h], ws_mx[half][h], slice(a * P, (a + 1) * P), slice(0, N_TILE),
+                    h == 0, h == H - 1,
                 )
 
-        out_view = out.rearrange("(p a) e -> p a e", a=A)
+        out_by_tile = out.rearrange("(r a) e -> r a e", a=A)
 
-        def finish(e):
-            e_cols = slice(e * 512, (e + 1) * 512)
+        def finish(half):
+            cols = slice(half * N_TILE, (half + 1) * N_TILE)
             for a in range(A):
-                nc.vector.tensor_tensor(out=resid[a][:, e_cols], in0=out_banks[(e, a)][:], in1=resid[a][:, e_cols], op=ADD)
-                nc.sync.dma_start(out=out_view[:, a, e_cols], in_=resid[a][:, e_cols])
+                nc.vector.tensor_tensor(
+                    out=residual[a][:, cols], in0=out_banks[(half, a)][:], in1=residual[a][:, cols], op=ADD
+                )
+                nc.sync.dma_start(out=out_by_tile[:, a, cols], in_=residual[a][:, cols])
 
-        transpose_h1(0)
-        regroup_w2(0, "vector")
-        quantise(w2_mx[0], w2_grouped[0])
-        regroup_w2(1, "vector")
-        quantise(h1_mx[0], h1_grouped[0])
-        quantise(w2_mx[1], w2_grouped[1])
-        transpose_h1(1)
-        stage1(0)
-        regroup_w2(2, "scalar")
-        transpose_h1(2)
-        regroup_w2(3, "scalar")
-        transpose_h1(3)
-        quantise(h1_mx[1], h1_grouped[1])
-        quantise(w2_mx[2], w2_grouped[2])
-        quantise(h1_mx[2], h1_grouped[2])
-        stage1(1)
-        quantise(w2_mx[3], w2_grouped[3])
-        quantise(h1_mx[3], h1_grouped[3])
-        stage1(2)
-        stage1(3)
+        prepare_head(0)
+        quantise_head(0)
+        prepare_head(1)
         for h in range(H):
-            regroup_ws(0, h)
-            quantise(ws_mx[0][h], ws_grouped[(0, h)])
-            stage2(0, h)
-        for h in range(H):
-            nc.vector.tensor_tensor(out=resid[h][:], in0=q_sb[:, h, :], in1=rep_sb[:, h, :], op=SUB)
-            regroup_ws(1, h)
-            quantise(ws_mx[1][h], ws_grouped[(1, h)])
-            stage2(1, h)
+            for a in range(A):
+                stage1(h, a)
+                if a == 0 and h > 0:
+                    quantise(z_mx[h - 1])
+                if a == 1 and h + 1 < H:
+                    quantise_head(h + 1)
+                if a == 1 and h + 2 < H:
+                    prepare_head(h + 2)
+
+        for half in range(E_HALVES):
+            for h in range(H):
+                if half == 1:
+                    nc.vector.tensor_tensor(out=residual[h][:], in0=q_raw[:, h, :], in1=rep_raw[:, h, :], op=SUBTRACT)
+                regroup_ws(half, h)
+                quantise(ws_mx[half][h])
+                if half == 0 and h == 0:
+                    quantise(z_mx[H - 1])
+                stage2(half, h)
         finish(0)
         finish(1)

@@ -19,7 +19,7 @@ N_TILE = 512
 E_HALVES = E // N_TILE
 FLOPS = 2 * N * H * M * G + 2 * N * H * G * E
 
-W2_HEADS_ON_VECTOR = (0, 1)
+W2_SHARED_HEADS = (0, 1)
 
 
 def tile_treehopnode_pb_kernel(tc, h1, W2, b2, Ws, q, rep, out):
@@ -100,10 +100,10 @@ def tile_treehopnode_pb_kernel(tc, h1, W2, b2, Ws, q, rep, out):
                 )
             regrouped = w2_mx[h]["grouped"][:].rearrange("p (t c j) -> p c j t", t=PACK, j=PACK)
             rows = w2_raw[h][:].rearrange("p j (c t) -> p c j t", t=PACK)
-            if h in W2_HEADS_ON_VECTOR:
-                nc.vector.tensor_copy(out=regrouped, in_=rows)
-            else:
-                nc.scalar.copy(out=regrouped, in_=rows)
+            scalar_from = P // 2 if h in W2_SHARED_HEADS else 0
+            if scalar_from > 0:
+                nc.vector.tensor_copy(out=regrouped[:, :scalar_from], in_=rows[:, :scalar_from])
+            nc.scalar.copy(out=regrouped[:, scalar_from:], in_=rows[:, scalar_from:])
 
         def quantise_head(h):
             quantise(h1_mx[h])
@@ -141,13 +141,12 @@ def tile_treehopnode_pb_kernel(tc, h1, W2, b2, Ws, q, rep, out):
 
         out_by_tile = out.rearrange("(r a) e -> r a e", a=A)
 
-        def finish(half):
+        def finish(half, a):
             cols = slice(half * N_TILE, (half + 1) * N_TILE)
-            for a in range(A):
-                nc.vector.tensor_tensor(
-                    out=residual[a][:, cols], in0=out_banks[(half, a)][:], in1=residual[a][:, cols], op=ADD
-                )
-                nc.sync.dma_start(out=out_by_tile[:, a, cols], in_=residual[a][:, cols])
+            nc.vector.tensor_tensor(
+                out=residual[a][:, cols], in0=out_banks[(half, a)][:], in1=residual[a][:, cols], op=ADD
+            )
+            nc.sync.dma_start(out=out_by_tile[:, a, cols], in_=residual[a][:, cols])
 
         prepare_head(0)
         quantise_head(0)
@@ -162,14 +161,17 @@ def tile_treehopnode_pb_kernel(tc, h1, W2, b2, Ws, q, rep, out):
                 if a == 1 and h + 2 < H:
                     prepare_head(h + 2)
 
-        for half in range(E_HALVES):
-            for h in range(H):
-                if half == 1:
-                    nc.vector.tensor_tensor(out=residual[h][:], in0=q_raw[:, h, :], in1=rep_raw[:, h, :], op=SUBTRACT)
-                regroup_ws(half, h)
-                quantise(ws_mx[half][h])
-                if half == 0 and h == 0:
-                    quantise(z_mx[H - 1])
-                stage2(half, h)
-        finish(0)
-        finish(1)
+        for h in range(H):
+            regroup_ws(0, h)
+            quantise(ws_mx[0][h])
+            if h == 0:
+                quantise(z_mx[H - 1])
+            stage2(0, h)
+        for i in range(H):
+            nc.vector.tensor_tensor(out=residual[i][:], in0=q_raw[:, i, :], in1=rep_raw[:, i, :], op=SUBTRACT)
+            regroup_ws(1, i)
+            quantise(ws_mx[1][i])
+            stage2(1, i)
+            finish(0, i)
+        for a in range(A):
+            finish(1, a)

@@ -32,7 +32,6 @@ def tile_treehopnode_pb_kernel(tc, h1, W2, b2, Ws, q, rep, out):
         identity = sbuf.tile([P, P], F32, name="identity")
         make_identity(nc, identity[:])
         bias = sbuf.tile([P, H, PACK], BF16, name="bias")
-        nc.scalar.dma_start(out=bias[:], in_=b2.rearrange("h (c t) -> c h t", t=PACK))
 
         h1_raw = [sbuf.tile([P, A, M], BF16, name="h1_raw%d" % h) for h in range(H)]
         w2_raw = [sbuf.tile([P, PACK, G], BF16, name="w2_raw%d" % h) for h in range(H)]
@@ -46,6 +45,8 @@ def tile_treehopnode_pb_kernel(tc, h1, W2, b2, Ws, q, rep, out):
                 out=w2_raw[h][:].rearrange("p (u e) g -> p u (e g)", u=2),
                 in_=W2[h].rearrange("(u p e) g -> p u (e g)", u=2, e=2),
             )
+            if h == 0:
+                nc.sync.dma_start(out=bias[:], in_=b2.rearrange("h (c t) -> c h t", t=PACK))
         for h in range(H):
             nc.sync.dma_start(
                 out=ws_raw[h][:].rearrange("p t e -> p (t e)"),

from contextlib import ExitStack

import concourse.mybir as mybir
from concourse.masks import make_identity

FP8X4 = mybir.dt.float8_e4m3fn_x4
BF16 = mybir.dt.bfloat16
F32 = mybir.dt.float32
U32 = mybir.dt.uint32
U8 = mybir.dt.uint8
ADD = mybir.AluOpType.add
SUBTRACT = mybir.AluOpType.subtract

P = 128
PACK = 4
N, E, G, M, H = 512, 1024, 512, 512, 4
A = N // P
N_TILE = 512
E_HALVES = E // N_TILE
FLOPS = 2 * N * H * M * G + 2 * N * H * G * E

W2_SHARED_HEADS = (0, 1)


def tile_treehopnode_pb_kernel(tc, h1, W2, b2, Ws, q, rep, out):
    nc = tc.nc
    with ExitStack() as ctx:
        sbuf = ctx.enter_context(tc.tile_pool(name="sbuf", bufs=1))
        psum = ctx.enter_context(tc.psum_pool(name="psum", bufs=1))
        ctx.enter_context(tc.manual_schedule())

        identity = sbuf.tile([P, P], F32, name="identity")
        make_identity(nc, identity[:])
        bias = sbuf.tile([P, H, PACK], BF16, name="bias")

        h1_raw = [sbuf.tile([P, A, M], BF16, name="h1_raw%d" % h) for h in range(H)]
        w2_raw = [sbuf.tile([P, PACK, G], BF16, name="w2_raw%d" % h) for h in range(H)]
        ws_raw = [sbuf.tile([P, PACK, E], BF16, name="ws_raw%d" % h) for h in range(H)]
        q_raw = sbuf.tile([P, A, E], BF16, name="q_raw")
        rep_raw = sbuf.tile([P, A, E], BF16, name="rep_raw")
        h1_by_tile = h1.rearrange("(r a) h m -> r a h m", a=A)
        for h in range(H):
            nc.sync.dma_start(out=h1_raw[h][:], in_=h1_by_tile[:, :, h, :])
            nc.sync.dma_start(
                out=w2_raw[h][:].rearrange("p (u e) g -> p u (e g)", u=2),
                in_=W2[h].rearrange("(u p e) g -> p u (e g)", u=2, e=2),
            )
            if h == 0:
                nc.sync.dma_start(out=bias[:], in_=b2.rearrange("h (c t) -> c h t", t=PACK))
        for h in range(H):
            nc.sync.dma_start(
                out=ws_raw[h][:].rearrange("p t e -> p (t e)"),
                in_=Ws[h * G : (h + 1) * G, :].rearrange("(p t) e -> p (t e)", t=PACK),
            )
        nc.sync.dma_start(out=q_raw[:].rearrange("r a e -> r (a e)"), in_=q.rearrange("(r a) e -> r (a e)", a=A))
        nc.sync.dma_start(out=rep_raw[:].rearrange("r a e -> r (a e)"), in_=rep.rearrange("(r a) e -> r (a e)", a=A))

        def mx_operand(name):
            return {
                "grouped": sbuf.tile([P, N_TILE * PACK], BF16, name=name + "_grouped", align_bytes=64),
                "words": sbuf.tile([P, N_TILE], U32, name=name + "_words", align_bytes=64),
                "scales": sbuf.tile([P, N_TILE], U8, name=name + "_scales", align_bytes=64),
            }

        h1_mx = [mx_operand("h1_%d" % h) for h in range(H)]
        w2_mx = [mx_operand("w2_%d" % h) for h in range(H)]
        z_mx = [mx_operand("z_%d" % h) for h in range(H)]
        ws_mx = [[mx_operand("ws_%d_%d" % (half, h)) for h in range(H)] for half in range(E_HALVES)]
        residual = [sbuf.tile([P, E], F32, name="residual%d" % a) for a in range(A)]

        def quantise(operand):
            nc.vector.quantize_mx(
                out=operand["words"][:].bitcast(FP8X4), scales=operand["scales"][:], in_=operand["grouped"][:]
            )

        def matmul_mx(acc, stationary, moving, stationary_cols, moving_cols, start, stop):
            nc.tensor.matmul_mx(
                out=acc,
                lhsT=stationary["words"][:, stationary_cols].bitcast(FP8X4),
                lhsT_scale=stationary["scales"][:, stationary_cols],
                rhs=moving["words"][:, moving_cols].bitcast(FP8X4),
                rhs_scale=moving["scales"][:, moving_cols],
                start=start,
                stop=stop,
            )

        def psum_bank(shape, bank):
            return psum.tile(shape, F32, name="bank", tag="bank%d" % bank)

        def prepare_head(h):
            pairs = h1_raw[h][:].rearrange("r a m -> r (a m)").bitcast(F32)
            grouped_pairs = h1_mx[h]["grouped"][:].bitcast(F32).rearrange("p (a r u) -> p a r u", a=A, u=2)
            for b in range(2):
                bank = psum_bank([P, 2, 2, P], (2 * h + b) % 4)
                for i in range(2):
                    for u in range(2):
                        first = (M // 2) * (2 * b + i) + P * u
                        nc.tensor.transpose(bank[:, i, u, :], pairs[:, first : first + P], identity[:])
                nc.scalar.copy(
                    out=grouped_pairs[:, 2 * b : 2 * b + 2, :, :], in_=bank[:].rearrange("p i u r -> p i r u")
                )
            regrouped = w2_mx[h]["grouped"][:].rearrange("p (t c j) -> p c j t", t=PACK, j=PACK)
            rows = w2_raw[h][:].rearrange("p j (c t) -> p c j t", t=PACK)
            scalar_from = P // 2 if h in W2_SHARED_HEADS else 0
            if scalar_from > 0:
                nc.vector.tensor_copy(out=regrouped[:, :scalar_from], in_=rows[:, :scalar_from])
            nc.scalar.copy(out=regrouped[:, scalar_from:], in_=rows[:, scalar_from:])

        def quantise_head(h):
            quantise(h1_mx[h])
            quantise(w2_mx[h])

        def stage1(h, a):
            bank = psum_bank([P, PACK, P], 4 + a)
            for t in range(PACK):
                matmul_mx(
                    bank[:, t, :], w2_mx[h], h1_mx[h], slice(t * P, (t + 1) * P), slice(a * P, (a + 1) * P), True, True
                )
            nc.vector.tensor_tensor(
                out=z_mx[h]["grouped"][:].rearrange("c (a r t) -> c a r t", a=A, t=PACK)[:, a, :, :],
                in0=bank[:].rearrange("c t r -> c r t"),
                in1=bias[:, h, :].unsqueeze(1).to_broadcast([P, P, PACK]),
                op=ADD,
            )

        def regroup_ws(half, h):
            nc.scalar.copy(
                out=ws_mx[half][h]["grouped"][:].rearrange("p (c i t) -> p c t i", i=4, t=PACK),
                in_=ws_raw[h][:, :, half * N_TILE : (half + 1) * N_TILE].rearrange("p t (c i) -> p c t i", i=4),
            )

        out_banks = {}

        def stage2(half, h):
            for a in range(A):
                if h == 0:
                    out_banks[(half, a)] = psum_bank([P, N_TILE], 4 * half + a)
                matmul_mx(
                    out_banks[(half, a)][:], z_mx[h], ws_mx[half][h], slice(a * P, (a + 1) * P), slice(0, N_TILE),
                    h == 0, h == H - 1,
                )

        out_by_tile = out.rearrange("(r a) e -> r a e", a=A)

        def finish(half, a):
            cols = slice(half * N_TILE, (half + 1) * N_TILE)
            nc.vector.tensor_tensor(
                out=residual[a][:, cols], in0=out_banks[(half, a)][:], in1=residual[a][:, cols], op=ADD
            )
            nc.sync.dma_start(out=out_by_tile[:, a, cols], in_=residual[a][:, cols])

        prepare_head(0)
        quantise_head(0)
        prepare_head(1)
        for h in range(H):
            for a in range(A):
                stage1(h, a)
                if a == 0 and h > 0:
                    quantise(z_mx[h - 1])
                if a == 1 and h + 1 < H:
                    quantise_head(h + 1)
                if a == 1 and h + 2 < H:
                    prepare_head(h + 2)

        for h in range(H):
            regroup_ws(0, h)
            quantise(ws_mx[0][h])
            if h == 0:
                quantise(z_mx[H - 1])
            stage2(0, h)
        for i in range(H):
            nc.vector.tensor_tensor(out=residual[i][:], in0=q_raw[:, i, :], in1=rep_raw[:, i, :], op=SUBTRACT)
            regroup_ws(1, i)
            quantise(ws_mx[1][i])
            stage2(1, i)
            finish(0, i)
        for a in range(A):
            finish(1, a)
